import numpy as np
import ml_dtypes


def mxq(x, axis, fmt="e4m3"):
    dtype, down = {"e4m3": (ml_dtypes.float8_e4m3fn, 7), "e5m2": (ml_dtypes.float8_e5m2, 14)}[fmt]
    v = np.moveaxis(np.asarray(x, np.float32).astype(ml_dtypes.bfloat16).astype(np.float64), axis, -1)
    blocks = v.reshape(v.shape[:-1] + (-1, 32))
    amax = np.abs(blocks).max(-1, keepdims=True)
    byte = np.maximum(np.where(amax > 0, np.frexp(amax)[1] - 1 + 127, 0) - down, 1)
    scale = np.exp2(byte - 127.0)
    codes = (blocks / scale).astype(np.float32).astype(dtype).astype(np.float64)
    return np.moveaxis((codes * scale).reshape(v.shape), -1, axis)


WIDE = False


def mx_kscale(k):
    if not WIDE:
        return np.ones(k)
    levels = np.array([10, -10, 5, -5, 0])
    a = np.random.permutation(np.resize(levels, k // 512 * 4)).reshape(k // 512, 4)
    idx = np.arange(k)
    return np.exp2(a[idx // 512, idx % 128 // 32])


BF16 = ml_dtypes.bfloat16


def bf(x):
    return np.asarray(x, np.float32).astype(BF16)


def f64(x):
    return np.asarray(x).astype(np.float64)


B, D, K = 640, 512, 4


def setup_inputs():
    s = mx_kscale(D)
    x = np.random.standard_normal((B, D, K)) * s[None, :, None]
    mu = np.random.standard_normal((D, K)) * 0.3 * s[:, None]
    w = (np.eye(D)[None] + np.random.standard_normal((K, D, D)) * 0.7 / np.sqrt(D)) / s[None, None, :]
    return {"x": bf(x), "mu_track": bf(mu), "Std_inv_track": bf(w)}


def reference(x, mu_track, Std_inv_track):
    x_cnt = f64(x) - f64(mu_track)[None]
    xq = mxq(x_cnt, 1, "e4m3")
    wq = mxq(f64(Std_inv_track), 2, "e4m3")
    z = wq @ xq.transpose(2, 1, 0)
    return z.transpose(2, 1, 0)

@@ -1,0 +1,151 @@
+from contextlib import ExitStack
+
+import concourse.mybir as mybir
+from concourse.masks import make_identity
+
+F32 = mybir.dt.float32
+BF16 = mybir.dt.bfloat16
+U32 = mybir.dt.uint32
+U8 = mybir.dt.uint8
+FP8X4 = mybir.dt.float8_e4m3fn_x4
+
+P = 128
+B, D, K = 640, 512, 4
+NB = B // P
+NC = D // P
+FLOPS = 2 * K * D * D * B
+
+LOADS = [
+    ("LX", 0), ("LW", 0), ("LW", 1), ("LX", 1), ("LW", 2), ("LW", 3),
+    ("LX", 2), ("LX", 3), ("LX", 4),
+]
+STEPS = [
+    ("TX", 0, 0), ("TX", 0, 1), ("F", 0, 0), ("TW", 0, 0), ("TW", 0, 1), ("F", 0, 1),
+    ("CW", 0, 0), ("CW", 0, 1), ("TW", 1, 0), ("QX", 0, 0, 2), ("TW", 1, 1), ("CW", 1, 0),
+    ("QW", 0), ("CW", 1, 1), ("TX", 1, 0), ("TX", 1, 1), ("QW", 1), ("MX", 0, 0, 0, 4),
+    ("F", 1, 0), ("MX", 0, 1, 0, 4), ("CO", 0, 0, "s"), ("TW", 2, 0), ("CO", 0, 1, "s"), ("TW", 2, 1),
+    ("F", 1, 1), ("TW", 3, 0), ("CW", 2, 0), ("ST", 0, 0, 1), ("CW", 2, 1), ("QX", 1, 0, 2),
+    ("TW", 3, 1), ("CW", 3, 0), ("QW", 2), ("MX", 1, 0, 0, 4), ("CW", 3, 1), ("MX", 1, 1, 0, 4),
+    ("CO", 1, 0, "s"), ("TX", 2, 0), ("QW", 3), ("CO", 1, 1, "s"), ("TX", 2, 1), ("F", 2, 0),
+    ("ST", 1, 0, 1), ("MX", 0, 2, 0, 4), ("MX", 0, 3, 0, 4), ("CO", 0, 2, "s"), ("MX", 1, 2, 0, 4), ("F", 2, 1),
+    ("MX", 1, 3, 0, 4), ("CO", 0, 3, "s"), ("TX", 3, 0), ("CO", 1, 2, "s"), ("ST", 0, 2, 3), ("TX", 3, 1),
+    ("QX", 2, 0, 2), ("CO", 1, 3, "s"), ("F", 3, 0), ("MX", 2, 0, 0, 4), ("ST", 1, 2, 3), ("MX", 2, 1, 0, 4),
+    ("CO", 2, 0, "s"), ("MX", 2, 2, 0, 4), ("F", 3, 1), ("MX", 2, 3, 0, 4), ("CO", 2, 1, "s"), ("TX", 4, 0),
+    ("CO", 2, 2, "s"), ("ST", 2, 0, 1), ("TX", 4, 1), ("QX", 3, 0, 2), ("CO", 2, 3, "s"), ("F", 4, 0),
+    ("ST", 2, 2, 3), ("MX", 3, 0, 0, 4), ("MX", 3, 1, 0, 4), ("CO", 3, 0, "s"), ("MX", 3, 2, 0, 4), ("QX", 4, 0, 1),
+    ("MX", 3, 3, 0, 4), ("CO", 3, 1, "s"), ("F", 4, 1), ("MX", 4, 0, 0, 2), ("CO", 3, 2, "s"), ("MX", 4, 1, 0, 2),
+    ("ST", 3, 0, 1), ("CO", 3, 3, "s"), ("MX", 4, 2, 0, 2), ("QX", 4, 1, 1), ("MX", 4, 3, 0, 2), ("ST", 3, 2, 3),
+    ("MX", 4, 0, 2, 2), ("MX", 4, 1, 2, 2), ("CO", 4, 0, "s"), ("MX", 4, 2, 2, 2), ("CO", 4, 1, "v"), ("MX", 4, 3, 2, 2),
+    ("CO", 4, 2, "s"), ("CO", 4, 3, "v"), ("ST", 4, 0, 1), ("ST", 4, 2, 2), ("ST", 4, 3, 3),
+]
+
+
+def tile_clusternorm1dv3_kernel(tc, x, mu_track, Std_inv_track, out):
+    nc = tc.nc
+    with ExitStack() as ctx:
+        keep = ctx.enter_context(tc.tile_pool(name="keep", bufs=1))
+        trp = ctx.enter_context(tc.psum_pool(name="trp", bufs=4))
+        accp = ctx.enter_context(tc.psum_pool(name="accp", bufs=4))
+        ctx.enter_context(tc.manual_schedule())
+
+        x_v = x.rearrange("(p i) e k -> i p (e k)", i=NB)
+        o_v = out.rearrange("(p i) d k -> i p (d k)", i=NB)
+        w_v = Std_inv_track.rearrange("k (c p) e -> c p k e", c=NC, p=P)
+        mu_v = mu_track.rearrange("(u p e) k -> p u (e k)", u=2, p=P, e=2)
+
+        ident = keep.tile([P, P], F32, name="ident")
+        make_identity(nc, ident[:])
+
+        mu_sb = keep.tile([P, 16], BF16, name="mu_sb")
+        nc.scalar.dma_start(out=mu_sb[:].rearrange("p (u c) -> p u c", u=2), in_=mu_v)
+
+        x_sb = [keep.tile([P, D * K], BF16, name="x%d" % i) for i in range(NB)]
+        w_sb = [keep.tile([P, K * D], BF16, name="w%d" % c) for c in range(NC)]
+        gx = [keep.tile([P, 2048], BF16, name="gx%d" % i, align_bytes=64) for i in range(NB)]
+        xc = [keep.tile([P, 512], U32, name="xc%d" % i, align_bytes=64) for i in range(NB)]
+        xs = [keep.tile([P, 512], U8, name="xs%d" % i, align_bytes=64) for i in range(NB)]
+        gw = [keep.tile([P, 2048], BF16, name="gw%d" % c, align_bytes=64) for c in range(NC)]
+        wc = [keep.tile([P, 512], U32, name="wc%d" % c, align_bytes=64) for c in range(NC)]
+        ws = [keep.tile([P, 512], U8, name="ws%d" % c, align_bytes=64) for c in range(NC)]
+        o_sb = [keep.tile([P, D * K], F32, name="o%d" % i) for i in range(NB)]
+        banks = {}
+
+        for step in LOADS:
+            if step[0] == "LX":
+                nc.sync.dma_start(out=x_sb[step[1]][:], in_=x_v[step[1]])
+            else:
+                nc.sync.dma_start(out=w_sb[step[1]][:].rearrange("p (k e) -> p k e", k=K), in_=w_v[step[1]])
+
+        for step in STEPS:
+            kind = step[0]
+            if kind == "TX":
+                i, h = step[1], step[2]
+                xw = x_sb[i][:].bitcast(F32).rearrange("b (u p e h) -> b u e h p", u=2, p=P, e=2, h=2)
+                bank = trp.tile([P, 512], F32, name="tr", tag="tr")
+                for t in range(4):
+                    nc.tensor.transpose(bank[:, t * P : (t + 1) * P], xw[:, t // 2, t % 2, h, :], ident[:])
+                banks[("X", i, h)] = bank
+            elif kind == "F":
+                i, h = step[1], step[2]
+                nc.vector.tensor_tensor(
+                    out=gx[i][:, h * 1024 : (h + 1) * 1024].rearrange("p (j b t) -> p j b t", j=2, b=P, t=4),
+                    in0=banks[("X", i, h)][:].bitcast(BF16).rearrange("p (t b j) -> p j b t", t=4, b=P, j=2),
+                    in1=mu_sb[:]
+                    .rearrange("p (t k) -> p k t", k=K)[:, 2 * h : 2 * h + 2, :]
+                    .unsqueeze(2)
+                    .to_broadcast([P, 2, P, 4]),
+                    op=mybir.AluOpType.subtract,
+                )
+            elif kind == "QX":
+                i, h, n = step[1], step[2], step[3]
+                nc.vector.quantize_mx(
+                    out=xc[i][:, h * 256 : (h + n) * 256].bitcast(FP8X4),
+                    scales=xs[i][:, h * 256 : (h + n) * 256],
+                    in_=gx[i][:, h * 1024 : (h + n) * 1024],
+                )
+            elif kind == "TW":
+                c, kp = step[1], step[2]
+                w32 = w_sb[c][:].bitcast(F32)
+                bank = trp.tile([P, 512], F32, name="tr", tag="tr")
+                for s in range(4):
+                    c0 = kp * 512 + s * P
+                    nc.tensor.transpose(bank[:, s * P : (s + 1) * P], w32[:, c0 : c0 + P], ident[:])
+                banks[("W", c, kp)] = bank
+            elif kind == "CW":
+                c, kp = step[1], step[2]
+                nc.scalar.copy(
+                    out=gw[c][:].bitcast(F32)[:, kp * 512 : (kp + 1) * 512].rearrange("p (k d u) -> p k d u", k=2, d=P, u=2),
+                    in_=banks[("W", c, kp)][:].rearrange("p (k u d) -> p k d u", k=2, u=2, d=P),
+                )
+            elif kind == "QW":
+                c = step[1]
+                nc.vector.quantize_mx(out=wc[c][:].bitcast(FP8X4), scales=ws[c][:], in_=gw[c][:])
+            elif kind == "MX":
+                i, c, k0, n = step[1], step[2], step[3], step[4]
+                if k0 == 0:
+                    acc = accp.tile([P, 512], F32, name="acc", tag="acc")
+                    banks[("A", i, c)] = acc
+                acc = banks[("A", i, c)]
+                for k in range(k0, k0 + n):
+                    cols = slice(k * P, (k + 1) * P)
+                    nc.tensor.matmul_mx(
+                        out=acc[:, cols],
+                        lhsT=xc[i][:, cols].bitcast(FP8X4),
+                        lhsT_scale=xs[i][:, cols],
+                        rhs=wc[c][:, cols].bitcast(FP8X4),
+                        rhs_scale=ws[c][:, cols],
+                        start=True,
+                        stop=True,
+                    )
+            elif kind == "CO":
+                i, c = step[1], step[2]
+                dst = o_sb[i][:, c * 512 : (c + 1) * 512].rearrange("p (d k) -> p d k", k=K)
+                src = banks[("A", i, c)][:].rearrange("p (k d) -> p d k", k=K)
+                if step[3] == "v":
+                    nc.vector.tensor_copy(out=dst, in_=src)
+                else:
+                    nc.scalar.copy(out=dst, in_=src)
+            else:
+                i, c0, c1 = step[1], step[2], step[3]
+                cols = slice(c0 * 512, (c1 + 1) * 512)
+                nc.sync.dma_start(out=o_v[i][:, cols], in_=o_sb[i][:, cols])

@@ -16,27 +16,27 @@ NC = D // P
 FLOPS = 2 * K * D * D * B
 
 LOADS = [
-    ("LX", 0), ("LW", 0), ("LW", 1), ("LX", 1), ("LW", 2), ("LW", 3),
-    ("LX", 2), ("LX", 3), ("LX", 4),
+    ("LX", 0), ("LW", 0), ("LW", 1), ("LX", 1), ("LX", 2), ("LW", 2),
+    ("LW", 3), ("LX", 3), ("LX", 4),
 ]
 STEPS = [
-    ("TX", 0, 0), ("TX", 0, 1), ("F", 0, 0), ("TW", 0, 0), ("TW", 0, 1), ("F", 0, 1),
-    ("CW", 0, 0), ("CW", 0, 1), ("TW", 1, 0), ("QX", 0, 0, 2), ("TW", 1, 1), ("CW", 1, 0),
-    ("QW", 0), ("CW", 1, 1), ("TX", 1, 0), ("TX", 1, 1), ("QW", 1), ("MX", 0, 0, 0, 4),
-    ("F", 1, 0), ("MX", 0, 1, 0, 4), ("CO", 0, 0, "s"), ("TW", 2, 0), ("CO", 0, 1, "s"), ("TW", 2, 1),
-    ("F", 1, 1), ("TW", 3, 0), ("CW", 2, 0), ("ST", 0, 0, 1), ("CW", 2, 1), ("QX", 1, 0, 2),
-    ("TW", 3, 1), ("CW", 3, 0), ("QW", 2), ("MX", 1, 0, 0, 4), ("CW", 3, 1), ("MX", 1, 1, 0, 4),
-    ("CO", 1, 0, "s"), ("TX", 2, 0), ("QW", 3), ("CO", 1, 1, "s"), ("TX", 2, 1), ("F", 2, 0),
-    ("ST", 1, 0, 1), ("MX", 0, 2, 0, 4), ("MX", 0, 3, 0, 4), ("CO", 0, 2, "s"), ("MX", 1, 2, 0, 4), ("F", 2, 1),
-    ("MX", 1, 3, 0, 4), ("CO", 0, 3, "s"), ("TX", 3, 0), ("CO", 1, 2, "s"), ("ST", 0, 2, 3), ("TX", 3, 1),
-    ("QX", 2, 0, 2), ("CO", 1, 3, "s"), ("F", 3, 0), ("MX", 2, 0, 0, 4), ("ST", 1, 2, 3), ("MX", 2, 1, 0, 4),
-    ("CO", 2, 0, "s"), ("MX", 2, 2, 0, 4), ("F", 3, 1), ("MX", 2, 3, 0, 4), ("CO", 2, 1, "s"), ("TX", 4, 0),
-    ("CO", 2, 2, "s"), ("ST", 2, 0, 1), ("TX", 4, 1), ("QX", 3, 0, 2), ("CO", 2, 3, "s"), ("F", 4, 0),
-    ("ST", 2, 2, 3), ("MX", 3, 0, 0, 4), ("MX", 3, 1, 0, 4), ("CO", 3, 0, "s"), ("MX", 3, 2, 0, 4), ("QX", 4, 0, 1),
-    ("MX", 3, 3, 0, 4), ("CO", 3, 1, "s"), ("F", 4, 1), ("MX", 4, 0, 0, 2), ("CO", 3, 2, "s"), ("MX", 4, 1, 0, 2),
-    ("ST", 3, 0, 1), ("CO", 3, 3, "s"), ("MX", 4, 2, 0, 2), ("QX", 4, 1, 1), ("MX", 4, 3, 0, 2), ("ST", 3, 2, 3),
-    ("MX", 4, 0, 2, 2), ("MX", 4, 1, 2, 2), ("CO", 4, 0, "s"), ("MX", 4, 2, 2, 2), ("CO", 4, 1, "v"), ("MX", 4, 3, 2, 2),
-    ("CO", 4, 2, "s"), ("CO", 4, 3, "v"), ("ST", 4, 0, 1), ("ST", 4, 2, 2), ("ST", 4, 3, 3),
+    ("TX", 0, 0), ("TX", 0, 1), ("F", 0, 0), ("TW", 0, 0), ("F", 0, 1), ("TW", 0, 1),
+    ("CW", 0, 0), ("TX", 1, 0), ("QX", 0, 0, 2), ("CW", 0, 1), ("TW", 1, 1), ("F", 1, 0),
+    ("TX", 1, 1), ("CW", 1, 1), ("TW", 1, 0), ("F", 1, 1), ("TW", 2, 1), ("CW", 1, 0),
+    ("TW", 2, 0), ("CW", 2, 1), ("QW", 0), ("TW", 3, 0), ("QW", 1), ("CW", 2, 0),
+    ("TW", 3, 1), ("TX", 2, 0), ("QX", 1, 0, 2), ("CW", 3, 0), ("MX", 0, 1, 0, 4), ("QW", 2),
+    ("CW", 3, 1), ("MX", 1, 0, 0, 4), ("TX", 2, 1), ("F", 2, 0), ("CO", 0, 1, "s"), ("MX", 0, 0, 0, 4),
+    ("CO", 1, 0, "s"), ("MX", 1, 1, 0, 4), ("MX", 1, 2, 0, 4), ("F", 2, 1), ("CO", 0, 0, "s"), ("ST", 0, 0, 1),
+    ("TX", 3, 0), ("TX", 3, 1), ("CO", 1, 2, "s"), ("QW", 3), ("MX", 0, 2, 0, 4), ("CO", 1, 1, "s"),
+    ("ST", 1, 0, 1), ("QX", 2, 0, 2), ("MX", 1, 3, 0, 4), ("CO", 0, 2, "s"), ("MX", 0, 3, 0, 4), ("F", 3, 1),
+    ("TX", 4, 0), ("CO", 1, 3, "s"), ("ST", 1, 2, 3), ("MX", 2, 3, 0, 4), ("CO", 0, 3, "s"), ("ST", 0, 2, 3),
+    ("MX", 2, 2, 0, 4), ("F", 3, 0), ("TX", 4, 1), ("CO", 2, 3, "s"), ("MX", 2, 1, 0, 4), ("MX", 2, 0, 0, 4),
+    ("CO", 2, 2, "s"), ("ST", 2, 2, 3), ("QX", 3, 0, 2), ("CO", 2, 1, "s"), ("F", 4, 0), ("MX", 3, 3, 0, 4),
+    ("CO", 2, 0, "s"), ("ST", 2, 0, 1), ("MX", 3, 2, 0, 4), ("MX", 3, 0, 0, 4), ("CO", 3, 3, "s"), ("MX", 3, 1, 0, 4),
+    ("F", 4, 1), ("CO", 3, 2, "s"), ("ST", 3, 2, 3), ("QX", 4, 0, 1), ("CO", 3, 0, "s"), ("QX", 4, 1, 1),
+    ("MX", 4, 3, 0, 2), ("CO", 3, 1, "v"), ("ST", 3, 0, 1), ("MX", 4, 2, 0, 2), ("MX", 4, 3, 2, 2), ("MX", 4, 1, 0, 2),
+    ("MX", 4, 0, 0, 2), ("MX", 4, 2, 2, 2), ("CO", 4, 3, "s"), ("ST", 4, 3, 3), ("MX", 4, 0, 2, 2), ("MX", 4, 1, 2, 2),
+    ("CO", 4, 2, "s"), ("ST", 4, 2, 2), ("CO", 4, 0, "v"), ("CO", 4, 1, "s"), ("ST", 4, 0, 1),
 ]
 
 

@@ -16,27 +16,29 @@ NC = D // P
 FLOPS = 2 * K * D * D * B
 
 LOADS = [
-    ("LX", 0), ("LW", 0), ("LW", 1), ("LX", 1), ("LX", 2), ("LW", 2),
-    ("LW", 3), ("LX", 3), ("LX", 4),
+    ("LX", 0), ("LW", 0), ("LW", 1), ("LX", 1), ("LW", 2), ("LW", 3),
+    ("LX", 2), ("LX", 3), ("LX", 4),
 ]
 STEPS = [
-    ("TX", 0, 0), ("TX", 0, 1), ("F", 0, 0), ("TW", 0, 0), ("F", 0, 1), ("TW", 0, 1),
-    ("CW", 0, 0), ("TX", 1, 0), ("QX", 0, 0, 2), ("CW", 0, 1), ("TW", 1, 1), ("F", 1, 0),
-    ("TX", 1, 1), ("CW", 1, 1), ("TW", 1, 0), ("F", 1, 1), ("TW", 2, 1), ("CW", 1, 0),
-    ("TW", 2, 0), ("CW", 2, 1), ("QW", 0), ("TW", 3, 0), ("QW", 1), ("CW", 2, 0),
-    ("TW", 3, 1), ("TX", 2, 0), ("QX", 1, 0, 2), ("CW", 3, 0), ("MX", 0, 1, 0, 4), ("QW", 2),
-    ("CW", 3, 1), ("MX", 1, 0, 0, 4), ("TX", 2, 1), ("F", 2, 0), ("CO", 0, 1, "s"), ("MX", 0, 0, 0, 4),
-    ("CO", 1, 0, "s"), ("MX", 1, 1, 0, 4), ("MX", 1, 2, 0, 4), ("F", 2, 1), ("CO", 0, 0, "s"), ("ST", 0, 0, 1),
-    ("TX", 3, 0), ("TX", 3, 1), ("CO", 1, 2, "s"), ("QW", 3), ("MX", 0, 2, 0, 4), ("CO", 1, 1, "s"),
-    ("ST", 1, 0, 1), ("QX", 2, 0, 2), ("MX", 1, 3, 0, 4), ("CO", 0, 2, "s"), ("MX", 0, 3, 0, 4), ("F", 3, 1),
-    ("TX", 4, 0), ("CO", 1, 3, "s"), ("ST", 1, 2, 3), ("MX", 2, 3, 0, 4), ("CO", 0, 3, "s"), ("ST", 0, 2, 3),
-    ("MX", 2, 2, 0, 4), ("F", 3, 0), ("TX", 4, 1), ("CO", 2, 3, "s"), ("MX", 2, 1, 0, 4), ("MX", 2, 0, 0, 4),
-    ("CO", 2, 2, "s"), ("ST", 2, 2, 3), ("QX", 3, 0, 2), ("CO", 2, 1, "s"), ("F", 4, 0), ("MX", 3, 3, 0, 4),
-    ("CO", 2, 0, "s"), ("ST", 2, 0, 1), ("MX", 3, 2, 0, 4), ("MX", 3, 0, 0, 4), ("CO", 3, 3, "s"), ("MX", 3, 1, 0, 4),
-    ("F", 4, 1), ("CO", 3, 2, "s"), ("ST", 3, 2, 3), ("QX", 4, 0, 1), ("CO", 3, 0, "s"), ("QX", 4, 1, 1),
-    ("MX", 4, 3, 0, 2), ("CO", 3, 1, "v"), ("ST", 3, 0, 1), ("MX", 4, 2, 0, 2), ("MX", 4, 3, 2, 2), ("MX", 4, 1, 0, 2),
-    ("MX", 4, 0, 0, 2), ("MX", 4, 2, 2, 2), ("CO", 4, 3, "s"), ("ST", 4, 3, 3), ("MX", 4, 0, 2, 2), ("MX", 4, 1, 2, 2),
-    ("CO", 4, 2, "s"), ("ST", 4, 2, 2), ("CO", 4, 0, "v"), ("CO", 4, 1, "s"), ("ST", 4, 0, 1),
+    ("TX", 0, 0), ("TX", 0, 1), ("F", 0, 0), ("TW", 0, 0), ("TW", 0, 1), ("F", 0, 1),
+    ("TW", 1, 0), ("CW", 0, 0), ("CW", 0, 1), ("TX", 1, 0), ("QX", 0, 0, 2), ("CW", 1, 0),
+    ("TW", 1, 1), ("QW", 0), ("TX", 1, 1), ("F", 1, 0), ("CW", 1, 1), ("TW", 2, 0),
+    ("CW", 2, 0), ("F", 1, 1), ("TW", 2, 1), ("MX", 0, 0, 0, 4), ("TW", 3, 0), ("CW", 2, 1),
+    ("QW", 1), ("TW", 3, 1), ("CO", 0, 0, "s"), ("ST", 0, 0, 0), ("TX", 2, 0), ("QX", 1, 0, 2),
+    ("CW", 3, 0), ("TX", 2, 1), ("QW", 2), ("MX", 0, 1, 0, 4), ("CW", 3, 1), ("F", 2, 0),
+    ("MX", 1, 0, 0, 4), ("MX", 1, 1, 0, 4), ("CO", 0, 1, "s"), ("ST", 0, 1, 1), ("MX", 0, 2, 0, 4), ("F", 2, 1),
+    ("CO", 1, 0, "s"), ("ST", 1, 0, 0), ("MX", 1, 2, 0, 4), ("TX", 3, 0), ("CO", 1, 1, "s"), ("ST", 1, 1, 1),
+    ("TX", 3, 1), ("QW", 3), ("CO", 0, 2, "s"), ("ST", 0, 2, 2), ("QX", 2, 0, 2), ("CO", 1, 2, "s"),
+    ("ST", 1, 2, 2), ("MX", 0, 3, 0, 4), ("MX", 1, 3, 0, 4), ("F", 3, 0), ("MX", 2, 0, 0, 4), ("CO", 0, 3, "s"),
+    ("ST", 0, 3, 3), ("MX", 2, 1, 0, 4), ("CO", 1, 3, "s"), ("ST", 1, 3, 3), ("MX", 2, 2, 0, 4), ("F", 3, 1),
+    ("CO", 2, 0, "s"), ("ST", 2, 0, 0), ("MX", 2, 3, 0, 4), ("TX", 4, 0), ("CO", 2, 1, "s"), ("ST", 2, 1, 1),
+    ("QX", 3, 0, 2), ("TX", 4, 1), ("CO", 2, 2, "s"), ("ST", 2, 2, 2), ("F", 4, 0), ("MX", 3, 0, 0, 4),
+    ("CO", 2, 3, "s"), ("ST", 2, 3, 3), ("MX", 3, 1, 0, 4), ("MX", 3, 2, 0, 4), ("CO", 3, 0, "s"), ("ST", 3, 0, 0),
+    ("MX", 3, 3, 0, 4), ("F", 4, 1), ("CO", 3, 1, "s"), ("ST", 3, 1, 1), ("QX", 4, 0, 1), ("CO", 3, 2, "s"),
+    ("ST", 3, 2, 2), ("QX", 4, 1, 1), ("MX", 4, 0, 0, 2), ("CO", 3, 3, "s"), ("ST", 3, 3, 3), ("MX", 4, 1, 0, 2),
+    ("MX", 4, 0, 2, 2), ("MX", 4, 1, 2, 2), ("MX", 4, 2, 0, 2), ("MX", 4, 3, 0, 2), ("CO", 4, 0, "v"), ("ST", 4, 0, 0),
+    ("CO", 4, 1, "s"), ("ST", 4, 1, 1), ("MX", 4, 2, 2, 2), ("MX", 4, 3, 2, 2), ("CO", 4, 2, "v"), ("ST", 4, 2, 2),
+    ("CO", 4, 3, "s"), ("ST", 4, 3, 3),
 ]
 
 

from contextlib import ExitStack

import concourse.mybir as mybir
from concourse.masks import make_identity

F32 = mybir.dt.float32
BF16 = mybir.dt.bfloat16
U32 = mybir.dt.uint32
U8 = mybir.dt.uint8
FP8X4 = mybir.dt.float8_e4m3fn_x4

P = 128
B, D, K = 640, 512, 4
NB = B // P
NC = D // P
FLOPS = 2 * K * D * D * B

LOADS = [
    ("LX", 0), ("LW", 0), ("LW", 1), ("LX", 1), ("LW", 2), ("LW", 3),
    ("LX", 2), ("LX", 3), ("LX", 4),
]
STEPS = [
    ("TX", 0, 0), ("TX", 0, 1), ("F", 0, 0), ("TW", 0, 0), ("TW", 0, 1), ("F", 0, 1),
    ("TW", 1, 0), ("CW", 0, 0), ("CW", 0, 1), ("TX", 1, 0), ("QX", 0, 0, 2), ("CW", 1, 0),
    ("TW", 1, 1), ("QW", 0), ("TX", 1, 1), ("F", 1, 0), ("CW", 1, 1), ("TW", 2, 0),
    ("CW", 2, 0), ("F", 1, 1), ("TW", 2, 1), ("MX", 0, 0, 0, 4), ("TW", 3, 0), ("CW", 2, 1),
    ("QW", 1), ("TW", 3, 1), ("CO", 0, 0, "s"), ("ST", 0, 0, 0), ("TX", 2, 0), ("QX", 1, 0, 2),
    ("CW", 3, 0), ("TX", 2, 1), ("QW", 2), ("MX", 0, 1, 0, 4), ("CW", 3, 1), ("F", 2, 0),
    ("MX", 1, 0, 0, 4), ("MX", 1, 1, 0, 4), ("CO", 0, 1, "s"), ("ST", 0, 1, 1), ("MX", 0, 2, 0, 4), ("F", 2, 1),
    ("CO", 1, 0, "s"), ("ST", 1, 0, 0), ("MX", 1, 2, 0, 4), ("TX", 3, 0), ("CO", 1, 1, "s"), ("ST", 1, 1, 1),
    ("TX", 3, 1), ("QW", 3), ("CO", 0, 2, "s"), ("ST", 0, 2, 2), ("QX", 2, 0, 2), ("CO", 1, 2, "s"),
    ("ST", 1, 2, 2), ("MX", 0, 3, 0, 4), ("MX", 1, 3, 0, 4), ("F", 3, 0), ("MX", 2, 0, 0, 4), ("CO", 0, 3, "s"),
    ("ST", 0, 3, 3), ("MX", 2, 1, 0, 4), ("CO", 1, 3, "s"), ("ST", 1, 3, 3), ("MX", 2, 2, 0, 4), ("F", 3, 1),
    ("CO", 2, 0, "s"), ("ST", 2, 0, 0), ("MX", 2, 3, 0, 4), ("TX", 4, 0), ("CO", 2, 1, "s"), ("ST", 2, 1, 1),
    ("QX", 3, 0, 2), ("TX", 4, 1), ("CO", 2, 2, "s"), ("ST", 2, 2, 2), ("F", 4, 0), ("MX", 3, 0, 0, 4),
    ("CO", 2, 3, "s"), ("ST", 2, 3, 3), ("MX", 3, 1, 0, 4), ("MX", 3, 2, 0, 4), ("CO", 3, 0, "s"), ("ST", 3, 0, 0),
    ("MX", 3, 3, 0, 4), ("F", 4, 1), ("CO", 3, 1, "s"), ("ST", 3, 1, 1), ("QX", 4, 0, 1), ("CO", 3, 2, "s"),
    ("ST", 3, 2, 2), ("QX", 4, 1, 1), ("MX", 4, 0, 0, 2), ("CO", 3, 3, "s"), ("ST", 3, 3, 3), ("MX", 4, 1, 0, 2),
    ("MX", 4, 0, 2, 2), ("MX", 4, 1, 2, 2), ("MX", 4, 2, 0, 2), ("MX", 4, 3, 0, 2), ("CO", 4, 0, "v"), ("ST", 4, 0, 0),
    ("CO", 4, 1, "s"), ("ST", 4, 1, 1), ("MX", 4, 2, 2, 2), ("MX", 4, 3, 2, 2), ("CO", 4, 2, "v"), ("ST", 4, 2, 2),
    ("CO", 4, 3, "s"), ("ST", 4, 3, 3),
]


def tile_clusternorm1dv3_kernel(tc, x, mu_track, Std_inv_track, out):
    nc = tc.nc
    with ExitStack() as ctx:
        keep = ctx.enter_context(tc.tile_pool(name="keep", bufs=1))
        trp = ctx.enter_context(tc.psum_pool(name="trp", bufs=4))
        accp = ctx.enter_context(tc.psum_pool(name="accp", bufs=4))
        ctx.enter_context(tc.manual_schedule())

        x_v = x.rearrange("(p i) e k -> i p (e k)", i=NB)
        o_v = out.rearrange("(p i) d k -> i p (d k)", i=NB)
        w_v = Std_inv_track.rearrange("k (c p) e -> c p k e", c=NC, p=P)
        mu_v = mu_track.rearrange("(u p e) k -> p u (e k)", u=2, p=P, e=2)

        ident = keep.tile([P, P], F32, name="ident")
        make_identity(nc, ident[:])

        mu_sb = keep.tile([P, 16], BF16, name="mu_sb")
        nc.scalar.dma_start(out=mu_sb[:].rearrange("p (u c) -> p u c", u=2), in_=mu_v)

        x_sb = [keep.tile([P, D * K], BF16, name="x%d" % i) for i in range(NB)]
        w_sb = [keep.tile([P, K * D], BF16, name="w%d" % c) for c in range(NC)]
        gx = [keep.tile([P, 2048], BF16, name="gx%d" % i, align_bytes=64) for i in range(NB)]
        xc = [keep.tile([P, 512], U32, name="xc%d" % i, align_bytes=64) for i in range(NB)]
        xs = [keep.tile([P, 512], U8, name="xs%d" % i, align_bytes=64) for i in range(NB)]
        gw = [keep.tile([P, 2048], BF16, name="gw%d" % c, align_bytes=64) for c in range(NC)]
        wc = [keep.tile([P, 512], U32, name="wc%d" % c, align_bytes=64) for c in range(NC)]
        ws = [keep.tile([P, 512], U8, name="ws%d" % c, align_bytes=64) for c in range(NC)]
        o_sb = [keep.tile([P, D * K], F32, name="o%d" % i) for i in range(NB)]
        banks = {}

        for step in LOADS:
            if step[0] == "LX":
                nc.sync.dma_start(out=x_sb[step[1]][:], in_=x_v[step[1]])
            else:
                nc.sync.dma_start(out=w_sb[step[1]][:].rearrange("p (k e) -> p k e", k=K), in_=w_v[step[1]])

        for step in STEPS:
            kind = step[0]
            if kind == "TX":
                i, h = step[1], step[2]
                xw = x_sb[i][:].bitcast(F32).rearrange("b (u p e h) -> b u e h p", u=2, p=P, e=2, h=2)
                bank = trp.tile([P, 512], F32, name="tr", tag="tr")
                for t in range(4):
                    nc.tensor.transpose(bank[:, t * P : (t + 1) * P], xw[:, t // 2, t % 2, h, :], ident[:])
                banks[("X", i, h)] = bank
            elif kind == "F":
                i, h = step[1], step[2]
                nc.vector.tensor_tensor(
                    out=gx[i][:, h * 1024 : (h + 1) * 1024].rearrange("p (j b t) -> p j b t", j=2, b=P, t=4),
                    in0=banks[("X", i, h)][:].bitcast(BF16).rearrange("p (t b j) -> p j b t", t=4, b=P, j=2),
                    in1=mu_sb[:]
                    .rearrange("p (t k) -> p k t", k=K)[:, 2 * h : 2 * h + 2, :]
                    .unsqueeze(2)
                    .to_broadcast([P, 2, P, 4]),
                    op=mybir.AluOpType.subtract,
                )
            elif kind == "QX":
                i, h, n = step[1], step[2], step[3]
                nc.vector.quantize_mx(
                    out=xc[i][:, h * 256 : (h + n) * 256].bitcast(FP8X4),
                    scales=xs[i][:, h * 256 : (h + n) * 256],
                    in_=gx[i][:, h * 1024 : (h + n) * 1024],
                )
            elif kind == "TW":
                c, kp = step[1], step[2]
                w32 = w_sb[c][:].bitcast(F32)
                bank = trp.tile([P, 512], F32, name="tr", tag="tr")
                for s in range(4):
                    c0 = kp * 512 + s * P
                    nc.tensor.transpose(bank[:, s * P : (s + 1) * P], w32[:, c0 : c0 + P], ident[:])
                banks[("W", c, kp)] = bank
            elif kind == "CW":
                c, kp = step[1], step[2]
                nc.scalar.copy(
                    out=gw[c][:].bitcast(F32)[:, kp * 512 : (kp + 1) * 512].rearrange("p (k d u) -> p k d u", k=2, d=P, u=2),
                    in_=banks[("W", c, kp)][:].rearrange("p (k u d) -> p k d u", k=2, u=2, d=P),
                )
            elif kind == "QW":
                c = step[1]
                nc.vector.quantize_mx(out=wc[c][:].bitcast(FP8X4), scales=ws[c][:], in_=gw[c][:])
            elif kind == "MX":
                i, c, k0, n = step[1], step[2], step[3], step[4]
                if k0 == 0:
                    acc = accp.tile([P, 512], F32, name="acc", tag="acc")
                    banks[("A", i, c)] = acc
                acc = banks[("A", i, c)]
                for k in range(k0, k0 + n):
                    cols = slice(k * P, (k + 1) * P)
                    nc.tensor.matmul_mx(
                        out=acc[:, cols],
                        lhsT=xc[i][:, cols].bitcast(FP8X4),
                        lhsT_scale=xs[i][:, cols],
                        rhs=wc[c][:, cols].bitcast(FP8X4),
                        rhs_scale=ws[c][:, cols],
                        start=True,
                        stop=True,
                    )
            elif kind == "CO":
                i, c = step[1], step[2]
                dst = o_sb[i][:, c * 512 : (c + 1) * 512].rearrange("p (d k) -> p d k", k=K)
                src = banks[("A", i, c)][:].rearrange("p (k d) -> p d k", k=K)
                if step[3] == "v":
                    nc.vector.tensor_copy(out=dst, in_=src)
                else:
                    nc.scalar.copy(out=dst, in_=src)
            else:
                i, c0, c1 = step[1], step[2], step[3]
                cols = slice(c0 * 512, (c1 + 1) * 512)
                nc.sync.dma_start(out=o_v[i][:, cols], in_=o_sb[i][:, cols])
